import numpy as np
import ml_dtypes


def mxq(x, axis, fmt="e4m3"):
    dtype, down = {"e4m3": (ml_dtypes.float8_e4m3fn, 7), "e5m2": (ml_dtypes.float8_e5m2, 14)}[fmt]
    v = np.moveaxis(np.asarray(x, np.float32).astype(ml_dtypes.bfloat16).astype(np.float64), axis, -1)
    blocks = v.reshape(v.shape[:-1] + (-1, 32))
    amax = np.abs(blocks).max(-1, keepdims=True)
    byte = np.maximum(np.where(amax > 0, np.frexp(amax)[1] - 1 + 127, 0) - down, 1)
    scale = np.exp2(byte - 127.0)
    codes = (blocks / scale).astype(np.float32).astype(dtype).astype(np.float64)
    return np.moveaxis((codes * scale).reshape(v.shape), -1, axis)


WIDE = False


def mx_kscale(k):
    if not WIDE:
        return np.ones(k)
    levels = np.array([20, -20, 10, -10, 0])
    a = np.random.permutation(np.resize(levels, k // 512 * 4)).reshape(k // 512, 4)
    idx = np.arange(k)
    return np.exp2(a[idx // 512, idx % 128 // 32])


BF16 = ml_dtypes.bfloat16


def bf(x):
    return np.asarray(x, np.float32).astype(BF16)


def f64(x):
    return np.asarray(x).astype(np.float64)


B, S, H, R = 4, 1024, 1024, 512
G = H // R


def setup_inputs():
    u = mx_kscale(R)
    x = np.random.standard_normal((B, S, H))
    matrix = np.random.standard_normal((R, R)) / np.sqrt(R) / u[None, :]
    g = (np.random.standard_normal((B, S, H)) * np.exp2(np.random.randint(-12, 1, (B, S, 1)))
         * 4.0 * np.repeat(u, G))
    return {"x": bf(x), "matrix": bf(matrix), "grad_out": bf(g)}


def reference(x, matrix, grad_out):
    matrix, g = f64(matrix), f64(grad_out)
    b, n, h = g.shape
    r = matrix.shape[0]
    grp = h // r
    gy = g.reshape(b, n, r, grp).sum(axis=3)
    gc = mxq(gy, 2, "e5m2") @ mxq(matrix, 1, "e4m3").T
    return np.tile(gc, (1, 1, grp))

@@ -1,0 +1,154 @@
+from contextlib import ExitStack
+
+import concourse.mybir as mybir
+from concourse.masks import make_identity
+
+F32 = mybir.dt.float32
+BF16 = mybir.dt.bfloat16
+U32 = mybir.dt.uint32
+U8 = mybir.dt.uint8
+E4M3X4 = mybir.dt.float8_e4m3fn_x4
+E5M2X4 = mybir.dt.float8_e5m2_x4
+
+P = 128
+TOKENS = 4096
+H = 1024
+R = 512
+T = TOKENS // P
+KC = R // P
+GP = 2
+NG = T // GP
+
+LOAD_SIZES = [1, 1, 2, 4, 8, 8, 8]
+STORE_SIZES = [4, 4, 4, 4, 4, 4, 4, 2, 2]
+
+FLOPS = 2 * TOKENS * R * R
+BYTES = TOKENS * H * 2 + R * R * 2 + TOKENS * H * 4
+
+
+def tile_mora_t_kernel(tc, x, matrix, grad_out, out):
+    nc = tc.nc
+    g_dram = grad_out.flatten_outer_dims().rearrange("(p t) h -> p t h", t=T)
+    o_dram = out.flatten_outer_dims().rearrange("(p t) h -> p t h", t=T)
+    m_dram = matrix.rearrange("(a r) k -> r a k", r=P)
+
+    with ExitStack() as ctx:
+        keep = ctx.enter_context(tc.tile_pool(name="keep", bufs=1))
+        work = ctx.enter_context(tc.tile_pool(name="work", bufs=3))
+        psum = ctx.enter_context(tc.psum_pool(name="psum", bufs=4))
+        ctx.enter_context(tc.manual_schedule())
+        ctx.enter_context(nc.allow_low_precision(reason="gy is rounded to bfloat16 once, as the task says"))
+
+        m_sb = keep.tile([P, KC, R], BF16, name="m_sb")
+        g_words = []
+        t0 = 0
+        for n, j in enumerate(LOAD_SIZES):
+            chunk = keep.tile([P, j, H], BF16, name="g%d" % n)
+            nc.sync.dma_start(out=chunk[:], in_=g_dram[:, t0 : t0 + j, :])
+            words = chunk[:].bitcast(F32)
+            for tl in range(j):
+                g_words.append((words, tl))
+            t0 += j
+            if n == 1:
+                nc.sync.dma_start(out=m_sb[:], in_=m_dram)
+
+        o_place = []
+        t0 = 0
+        for n, j in enumerate(STORE_SIZES):
+            oc = keep.tile([P, j, H], F32, name="o%d" % n)
+            for tl in range(j):
+                o_place.append((oc, tl, t0, j))
+            t0 += j
+
+        ident_f = keep.tile([P, P], F32, name="ident_f")
+        make_identity(nc, ident_f[:])
+        ident_b = keep.tile([P, P], BF16, name="ident_b")
+        make_identity(nc, ident_b[:])
+
+        m_grouped = keep.tile([P, R, KC], BF16, name="m_grouped", align_bytes=64)
+        m_codes = keep.tile([P, R], U32, name="m_codes", align_bytes=64)
+        m_scales = keep.tile([P, R], U8, name="m_scales", align_bytes=64)
+
+        xts = {}
+        groupeds = {}
+        quants = {}
+
+        def transposes(g):
+            for n in range(GP):
+                words, tl = g_words[GP * g + n]
+                xt = psum.tile([P, KC, P], F32, tag="xt", name="xt")
+                for c in range(KC):
+                    nc.tensor.transpose(xt[:, c, :], words[:, tl, c * P : (c + 1) * P], ident_f[:])
+                xts[(g, n)] = xt
+
+        def pair_sums(g):
+            grouped = work.tile([P, GP, P, KC], BF16, tag="grouped", name="grouped", align_bytes=64)
+            for n in range(GP):
+                pairs = xts[(g, n)][:].bitcast(BF16).rearrange("q c (p e) -> q p c e", e=2)
+                nc.vector.tensor_reduce(
+                    out=grouped[:, n, :, :], in_=pairs, axis=mybir.AxisListType.X, op=mybir.AluOpType.add
+                )
+            groupeds[g] = grouped
+
+        def quantise(g):
+            codes = work.tile([P, GP * P], U32, tag="codes", name="codes", align_bytes=64)
+            scales = work.tile([P, GP * P], U8, tag="scales", name="scales", align_bytes=64)
+            nc.vector.quantize_mx(
+                out=codes[:].bitcast(E5M2X4),
+                scales=scales[:],
+                in_=groupeds[g][:].rearrange("q n p c -> q (n p c)"),
+            )
+            quants[g] = (codes, scales)
+
+        def multiply_and_store(g):
+            codes, scales = quants[g]
+            accs = []
+            for n in range(GP):
+                acc = psum.tile([P, R], F32, tag="acc", name="acc")
+                nc.tensor.matmul_mx(
+                    out=acc[:],
+                    lhsT=codes[:, n * P : (n + 1) * P].bitcast(E5M2X4),
+                    lhsT_scale=scales[:, n * P : (n + 1) * P],
+                    rhs=m_codes[:].bitcast(E4M3X4),
+                    rhs_scale=m_scales[:],
+                    start=True,
+                    stop=True,
+                )
+                accs.append(acc)
+            for n in range(GP):
+                oc, tl, first, size = o_place[GP * g + n]
+                nc.scalar.copy(
+                    out=oc[:, tl, :].rearrange("p (r i) -> p r i", r=2),
+                    in_=accs[n][:].unsqueeze(1).to_broadcast([P, 2, R]),
+                )
+                if tl == size - 1:
+                    nc.sync.dma_start(out=o_dram[:, first : first + size, :], in_=oc[:])
+
+        transposes(0)
+        transposes(1)
+        for h in range(2):
+            mt = psum.tile([P, 2, KC, P], BF16, tag="acc", name="mt")
+            for a in range(2):
+                for c in range(KC):
+                    nc.tensor.transpose(mt[:, a, c, :], m_sb[:, 2 * h + a, c * P : (c + 1) * P], ident_b[:])
+            nc.scalar.copy(
+                out=m_grouped[:, 2 * P * h : 2 * P * (h + 1), :].rearrange("q (a r) c -> q a r c", a=2),
+                in_=mt[:].rearrange("q a c r -> q a r c"),
+            )
+        pair_sums(0)
+        transposes(2)
+        pair_sums(1)
+        nc.vector.quantize_mx(
+            out=m_codes[:].bitcast(E4M3X4), scales=m_scales[:], in_=m_grouped[:].rearrange("q i c -> q (i c)")
+        )
+        quantise(0)
+        multiply_and_store(0)
+        transposes(3)
+        for g in range(2, NG):
+            pair_sums(g)
+            quantise(g - 1)
+            multiply_and_store(g - 1)
+            if g + 2 < NG:
+                transposes(g + 2)
+        quantise(NG - 1)
+        multiply_and_store(NG - 1)

@@ -70,8 +70,10 @@ def tile_mora_t_kernel(tc, x, matrix, grad_out, out):
         m_scales = keep.tile([P, R], U8, name="m_scales", align_bytes=64)
 
         xts = {}
+        odds = {}
         groupeds = {}
         quants = {}
+        accs = {}
 
         def transposes(g):
             for n in range(GP):
@@ -79,14 +81,19 @@ def tile_mora_t_kernel(tc, x, matrix, grad_out, out):
                 xt = psum.tile([P, KC, P], F32, tag="xt", name="xt")
                 for c in range(KC):
                     nc.tensor.transpose(xt[:, c, :], words[:, tl, c * P : (c + 1) * P], ident_f[:])
-                xts[(g, n)] = xt
+                xts[(g, n)] = xt[:].bitcast(BF16).rearrange("q c (p e) -> q e p c", e=2)
+
+        def odd_halves(g):
+            odd = work.tile([P, GP, P, KC], BF16, tag="odd", name="odd")
+            for n in range(GP):
+                nc.scalar.copy(out=odd[:, n, :, :], in_=xts[(g, n)][:, 1, :, :])
+            odds[g] = odd
 
         def pair_sums(g):
             grouped = work.tile([P, GP, P, KC], BF16, tag="grouped", name="grouped", align_bytes=64)
             for n in range(GP):
-                pairs = xts[(g, n)][:].bitcast(BF16).rearrange("q c (p e) -> q p c e", e=2)
-                nc.vector.tensor_reduce(
-                    out=grouped[:, n, :, :], in_=pairs, axis=mybir.AxisListType.X, op=mybir.AluOpType.add
+                nc.vector.tensor_tensor(
+                    out=grouped[:, n, :, :], in0=xts[(g, n)][:, 0, :, :], in1=odds[g][:, n, :, :], op=mybir.AluOpType.add
                 )
             groupeds[g] = grouped
 
@@ -100,9 +107,8 @@ def tile_mora_t_kernel(tc, x, matrix, grad_out, out):
             )
             quants[g] = (codes, scales)
 
-        def multiply_and_store(g):
+        def multiply(g):
             codes, scales = quants[g]
-            accs = []
             for n in range(GP):
                 acc = psum.tile([P, R], F32, tag="acc", name="acc")
                 nc.tensor.matmul_mx(
@@ -114,41 +120,56 @@ def tile_mora_t_kernel(tc, x, matrix, grad_out, out):
                     start=True,
                     stop=True,
                 )
-                accs.append(acc)
+                accs[(g, n)] = acc
+
+        def empty_banks(g):
             for n in range(GP):
                 oc, tl, first, size = o_place[GP * g + n]
-                nc.scalar.copy(
-                    out=oc[:, tl, :].rearrange("p (r i) -> p r i", r=2),
-                    in_=accs[n][:].unsqueeze(1).to_broadcast([P, 2, R]),
+                nc.scalar.copy(out=oc[:, tl, 0:R], in_=accs[(g, n)][:])
+
+        def second_half_and_store(g):
+            oc, tl, first, size = o_place[GP * g]
+            nc.vector.tensor_copy(out=oc[:, tl : tl + GP, R:H], in_=oc[:, tl : tl + GP, 0:R])
+            if tl + GP == size:
+                nc.sync.dma_start(out=o_dram[:, first : first + size, :], in_=oc[:])
+
+        def matrix_transposes():
+            mts = []
+            for h in range(2):
+                mt = psum.tile([P, 2, KC, P], BF16, tag="acc", name="mt")
+                for a in range(2):
+                    for c in range(KC):
+                        nc.tensor.transpose(mt[:, a, c, :], m_sb[:, 2 * h + a, c * P : (c + 1) * P], ident_b[:])
+                mts.append(mt)
+            return mts
+
+        def matrix_quantise(mts):
+            for h in range(2):
+                nc.vector.tensor_copy(
+                    out=m_grouped[:, 2 * P * h : 2 * P * (h + 1), :].rearrange("q (a r) c -> q a r c", a=2),
+                    in_=mts[h][:].rearrange("q a c r -> q a r c"),
                 )
-                if tl == size - 1:
-                    nc.sync.dma_start(out=o_dram[:, first : first + size, :], in_=oc[:])
+            nc.vector.quantize_mx(
+                out=m_codes[:].bitcast(E4M3X4), scales=m_scales[:], in_=m_grouped[:].rearrange("q i c -> q (i c)")
+            )
 
         transposes(0)
+        odd_halves(0)
+        mts = matrix_transposes()
         transposes(1)
-        for h in range(2):
-            mt = psum.tile([P, 2, KC, P], BF16, tag="acc", name="mt")
-            for a in range(2):
-                for c in range(KC):
-                    nc.tensor.transpose(mt[:, a, c, :], m_sb[:, 2 * h + a, c * P : (c + 1) * P], ident_b[:])
-            nc.scalar.copy(
-                out=m_grouped[:, 2 * P * h : 2 * P * (h + 1), :].rearrange("q (a r) c -> q a r c", a=2),
-                in_=mt[:].rearrange("q a c r -> q a r c"),
-            )
-        pair_sums(0)
-        transposes(2)
-        pair_sums(1)
-        nc.vector.quantize_mx(
-            out=m_codes[:].bitcast(E4M3X4), scales=m_scales[:], in_=m_grouped[:].rearrange("q i c -> q (i c)")
-        )
-        quantise(0)
-        multiply_and_store(0)
-        transposes(3)
-        for g in range(2, NG):
-            pair_sums(g)
-            quantise(g - 1)
-            multiply_and_store(g - 1)
-            if g + 2 < NG:
-                transposes(g + 2)
-        quantise(NG - 1)
-        multiply_and_store(NG - 1)
+        for i in range(NG + 2):
+            if i + 1 < NG:
+                odd_halves(i + 1)
+            if 1 <= i <= NG:
+                empty_banks(i - 1)
+            if i < NG:
+                pair_sums(i)
+            if i + 2 < NG:
+                transposes(i + 2)
+            if i == 0:
+                matrix_quantise(mts)
+            if i >= 2:
+                second_half_and_store(i - 2)
+            if i < NG:
+                quantise(i)
+                multiply(i)

@@ -19,8 +19,8 @@ KC = R // P
 GP = 2
 NG = T // GP
 
-LOAD_SIZES = [1, 1, 2, 4, 8, 8, 8]
-STORE_SIZES = [4, 4, 4, 4, 4, 4, 4, 2, 2]
+LOAD_SIZES = [2, 2, 4, 8, 16]
+STORE_SIZES = [4, 4, 4, 4, 4, 4, 4, 4]
 
 FLOPS = 2 * TOKENS * R * R
 BYTES = TOKENS * H * 2 + R * R * 2 + TOKENS * H * 4
@@ -30,7 +30,7 @@ def tile_mora_t_kernel(tc, x, matrix, grad_out, out):
     nc = tc.nc
     g_dram = grad_out.flatten_outer_dims().rearrange("(p t) h -> p t h", t=T)
     o_dram = out.flatten_outer_dims().rearrange("(p t) h -> p t h", t=T)
-    m_dram = matrix.rearrange("(a r) k -> r a k", r=P)
+    m_dram = matrix.rearrange("(r a) k -> r a k", r=P)
 
     with ExitStack() as ctx:
         keep = ctx.enter_context(tc.tile_pool(name="keep", bufs=1))
@@ -40,6 +40,7 @@ def tile_mora_t_kernel(tc, x, matrix, grad_out, out):
         ctx.enter_context(nc.allow_low_precision(reason="gy is rounded to bfloat16 once, as the task says"))
 
         m_sb = keep.tile([P, KC, R], BF16, name="m_sb")
+        nc.sync.dma_start(out=m_sb[:], in_=m_dram)
         g_words = []
         t0 = 0
         for n, j in enumerate(LOAD_SIZES):
@@ -49,8 +50,6 @@ def tile_mora_t_kernel(tc, x, matrix, grad_out, out):
             for tl in range(j):
                 g_words.append((words, tl))
             t0 += j
-            if n == 1:
-                nc.sync.dma_start(out=m_sb[:], in_=m_dram)
 
         o_place = []
         t0 = 0
@@ -146,16 +145,16 @@ def tile_mora_t_kernel(tc, x, matrix, grad_out, out):
         def matrix_quantise(mts):
             for h in range(2):
                 nc.vector.tensor_copy(
-                    out=m_grouped[:, 2 * P * h : 2 * P * (h + 1), :].rearrange("q (a r) c -> q a r c", a=2),
-                    in_=mts[h][:].rearrange("q a c r -> q a r c"),
+                    out=m_grouped[:].rearrange("q (r a) c -> q r a c", a=4)[:, :, 2 * h : 2 * h + 2, :],
+                    in_=mts[h][:].rearrange("q a c r -> q r a c"),
                 )
             nc.vector.quantize_mx(
                 out=m_codes[:].bitcast(E4M3X4), scales=m_scales[:], in_=m_grouped[:].rearrange("q i c -> q (i c)")
             )
 
+        matrix_quantise(matrix_transposes())
         transposes(0)
         odd_halves(0)
-        mts = matrix_transposes()
         transposes(1)
         for i in range(NG + 2):
             if i + 1 < NG:
@@ -166,8 +165,6 @@ def tile_mora_t_kernel(tc, x, matrix, grad_out, out):
                 pair_sums(i)
             if i + 2 < NG:
                 transposes(i + 2)
-            if i == 0:
-                matrix_quantise(mts)
             if i >= 2:
                 second_half_and_store(i - 2)
             if i < NG:

@@ -21,6 +21,7 @@ NG = T // GP
 
 LOAD_SIZES = [2, 2, 4, 8, 16]
 STORE_SIZES = [4, 4, 4, 4, 4, 4, 4, 4]
+DMA_ALIGN = 512
 
 FLOPS = 2 * TOKENS * R * R
 BYTES = TOKENS * H * 2 + R * R * 2 + TOKENS * H * 4
@@ -39,12 +40,12 @@ def tile_mora_t_kernel(tc, x, matrix, grad_out, out):
         ctx.enter_context(tc.manual_schedule())
         ctx.enter_context(nc.allow_low_precision(reason="gy is rounded to bfloat16 once, as the task says"))
 
-        m_sb = keep.tile([P, KC, R], BF16, name="m_sb")
+        m_sb = keep.tile([P, KC, R], BF16, name="m_sb", align_bytes=DMA_ALIGN)
         nc.sync.dma_start(out=m_sb[:], in_=m_dram)
         g_words = []
         t0 = 0
         for n, j in enumerate(LOAD_SIZES):
-            chunk = keep.tile([P, j, H], BF16, name="g%d" % n)
+            chunk = keep.tile([P, j, H], BF16, name="g%d" % n, align_bytes=DMA_ALIGN)
             nc.sync.dma_start(out=chunk[:], in_=g_dram[:, t0 : t0 + j, :])
             words = chunk[:].bitcast(F32)
             for tl in range(j):
@@ -54,7 +55,7 @@ def tile_mora_t_kernel(tc, x, matrix, grad_out, out):
         o_place = []
         t0 = 0
         for n, j in enumerate(STORE_SIZES):
-            oc = keep.tile([P, j, H], F32, name="o%d" % n)
+            oc = keep.tile([P, j, H], F32, name="o%d" % n, align_bytes=DMA_ALIGN)
             for tl in range(j):
                 o_place.append((oc, tl, t0, j))
             t0 += j

from contextlib import ExitStack

import concourse.mybir as mybir
from concourse.masks import make_identity

F32 = mybir.dt.float32
BF16 = mybir.dt.bfloat16
U32 = mybir.dt.uint32
U8 = mybir.dt.uint8
E4M3X4 = mybir.dt.float8_e4m3fn_x4
E5M2X4 = mybir.dt.float8_e5m2_x4

P = 128
TOKENS = 4096
H = 1024
R = 512
T = TOKENS // P
KC = R // P
GP = 2
NG = T // GP

LOAD_SIZES = [2, 2, 4, 8, 16]
STORE_SIZES = [4, 4, 4, 4, 4, 4, 4, 4]
DMA_ALIGN = 512

FLOPS = 2 * TOKENS * R * R
BYTES = TOKENS * H * 2 + R * R * 2 + TOKENS * H * 4


def tile_mora_t_kernel(tc, x, matrix, grad_out, out):
    nc = tc.nc
    g_dram = grad_out.flatten_outer_dims().rearrange("(p t) h -> p t h", t=T)
    o_dram = out.flatten_outer_dims().rearrange("(p t) h -> p t h", t=T)
    m_dram = matrix.rearrange("(r a) k -> r a k", r=P)

    with ExitStack() as ctx:
        keep = ctx.enter_context(tc.tile_pool(name="keep", bufs=1))
        work = ctx.enter_context(tc.tile_pool(name="work", bufs=3))
        psum = ctx.enter_context(tc.psum_pool(name="psum", bufs=4))
        ctx.enter_context(tc.manual_schedule())
        ctx.enter_context(nc.allow_low_precision(reason="gy is rounded to bfloat16 once, as the task says"))

        m_sb = keep.tile([P, KC, R], BF16, name="m_sb", align_bytes=DMA_ALIGN)
        nc.sync.dma_start(out=m_sb[:], in_=m_dram)
        g_words = []
        t0 = 0
        for n, j in enumerate(LOAD_SIZES):
            chunk = keep.tile([P, j, H], BF16, name="g%d" % n, align_bytes=DMA_ALIGN)
            nc.sync.dma_start(out=chunk[:], in_=g_dram[:, t0 : t0 + j, :])
            words = chunk[:].bitcast(F32)
            for tl in range(j):
                g_words.append((words, tl))
            t0 += j

        o_place = []
        t0 = 0
        for n, j in enumerate(STORE_SIZES):
            oc = keep.tile([P, j, H], F32, name="o%d" % n, align_bytes=DMA_ALIGN)
            for tl in range(j):
                o_place.append((oc, tl, t0, j))
            t0 += j

        ident_f = keep.tile([P, P], F32, name="ident_f")
        make_identity(nc, ident_f[:])
        ident_b = keep.tile([P, P], BF16, name="ident_b")
        make_identity(nc, ident_b[:])

        m_grouped = keep.tile([P, R, KC], BF16, name="m_grouped", align_bytes=64)
        m_codes = keep.tile([P, R], U32, name="m_codes", align_bytes=64)
        m_scales = keep.tile([P, R], U8, name="m_scales", align_bytes=64)

        xts = {}
        odds = {}
        groupeds = {}
        quants = {}
        accs = {}

        def transposes(g):
            for n in range(GP):
                words, tl = g_words[GP * g + n]
                xt = psum.tile([P, KC, P], F32, tag="xt", name="xt")
                for c in range(KC):
                    nc.tensor.transpose(xt[:, c, :], words[:, tl, c * P : (c + 1) * P], ident_f[:])
                xts[(g, n)] = xt[:].bitcast(BF16).rearrange("q c (p e) -> q e p c", e=2)

        def odd_halves(g):
            odd = work.tile([P, GP, P, KC], BF16, tag="odd", name="odd")
            for n in range(GP):
                nc.scalar.copy(out=odd[:, n, :, :], in_=xts[(g, n)][:, 1, :, :])
            odds[g] = odd

        def pair_sums(g):
            grouped = work.tile([P, GP, P, KC], BF16, tag="grouped", name="grouped", align_bytes=64)
            for n in range(GP):
                nc.vector.tensor_tensor(
                    out=grouped[:, n, :, :], in0=xts[(g, n)][:, 0, :, :], in1=odds[g][:, n, :, :], op=mybir.AluOpType.add
                )
            groupeds[g] = grouped

        def quantise(g):
            codes = work.tile([P, GP * P], U32, tag="codes", name="codes", align_bytes=64)
            scales = work.tile([P, GP * P], U8, tag="scales", name="scales", align_bytes=64)
            nc.vector.quantize_mx(
                out=codes[:].bitcast(E5M2X4),
                scales=scales[:],
                in_=groupeds[g][:].rearrange("q n p c -> q (n p c)"),
            )
            quants[g] = (codes, scales)

        def multiply(g):
            codes, scales = quants[g]
            for n in range(GP):
                acc = psum.tile([P, R], F32, tag="acc", name="acc")
                nc.tensor.matmul_mx(
                    out=acc[:],
                    lhsT=codes[:, n * P : (n + 1) * P].bitcast(E5M2X4),
                    lhsT_scale=scales[:, n * P : (n + 1) * P],
                    rhs=m_codes[:].bitcast(E4M3X4),
                    rhs_scale=m_scales[:],
                    start=True,
                    stop=True,
                )
                accs[(g, n)] = acc

        def empty_banks(g):
            for n in range(GP):
                oc, tl, first, size = o_place[GP * g + n]
                nc.scalar.copy(out=oc[:, tl, 0:R], in_=accs[(g, n)][:])

        def second_half_and_store(g):
            oc, tl, first, size = o_place[GP * g]
            nc.vector.tensor_copy(out=oc[:, tl : tl + GP, R:H], in_=oc[:, tl : tl + GP, 0:R])
            if tl + GP == size:
                nc.sync.dma_start(out=o_dram[:, first : first + size, :], in_=oc[:])

        def matrix_transposes():
            mts = []
            for h in range(2):
                mt = psum.tile([P, 2, KC, P], BF16, tag="acc", name="mt")
                for a in range(2):
                    for c in range(KC):
                        nc.tensor.transpose(mt[:, a, c, :], m_sb[:, 2 * h + a, c * P : (c + 1) * P], ident_b[:])
                mts.append(mt)
            return mts

        def matrix_quantise(mts):
            for h in range(2):
                nc.vector.tensor_copy(
                    out=m_grouped[:].rearrange("q (r a) c -> q r a c", a=4)[:, :, 2 * h : 2 * h + 2, :],
                    in_=mts[h][:].rearrange("q a c r -> q r a c"),
                )
            nc.vector.quantize_mx(
                out=m_codes[:].bitcast(E4M3X4), scales=m_scales[:], in_=m_grouped[:].rearrange("q i c -> q (i c)")
            )

        matrix_quantise(matrix_transposes())
        transposes(0)
        odd_halves(0)
        transposes(1)
        for i in range(NG + 2):
            if i + 1 < NG:
                odd_halves(i + 1)
            if 1 <= i <= NG:
                empty_banks(i - 1)
            if i < NG:
                pair_sums(i)
            if i + 2 < NG:
                transposes(i + 2)
            if i >= 2:
                second_half_and_store(i - 2)
            if i < NG:
                quantise(i)
                multiply(i)
